import numpy as np
import ml_dtypes


def mxq(x, axis, fmt="e4m3"):
    dtype, down = {"e4m3": (ml_dtypes.float8_e4m3fn, 7), "e5m2": (ml_dtypes.float8_e5m2, 14)}[fmt]
    v = np.moveaxis(np.asarray(x, np.float32).astype(ml_dtypes.bfloat16).astype(np.float64), axis, -1)
    blocks = v.reshape(v.shape[:-1] + (-1, 32))
    amax = np.abs(blocks).max(-1, keepdims=True)
    byte = np.maximum(np.where(amax > 0, np.frexp(amax)[1] - 1 + 127, 0) - down, 1)
    scale = np.exp2(byte - 127.0)
    codes = (blocks / scale).astype(np.float32).astype(dtype).astype(np.float64)
    return np.moveaxis((codes * scale).reshape(v.shape), -1, axis)


WIDE = False


def mx_kscale(k):
    if not WIDE:
        return np.ones(k)
    levels = np.array([10, -10, 5, -5, 0])
    a = np.random.permutation(np.resize(levels, k // 512 * 4)).reshape(k // 512, 4)
    idx = np.arange(k)
    return np.exp2(a[idx // 512, idx % 128 // 32])


BF16 = ml_dtypes.bfloat16


def bf(x):
    return np.asarray(x, np.float32).astype(BF16)


def f64(x):
    return np.asarray(x).astype(np.float64)


B, S, E, H, D, XL, TOPK = 2, 256, 1024, 8, 128, 512, 8
HD = H * D


def l2norm(x):
    return x / np.maximum(np.sqrt((x * x).sum(-1, keepdims=True)), 1e-12)


def split_heads(x):
    return x.reshape(B, S, H, D).transpose(0, 2, 1, 3)


def setup_inputs():
    n = np.random.standard_normal
    s = mx_kscale(E)
    return {"input": bf(n((B, S, E)) * s),
            "Wq": bf(n((HD, E)) / np.sqrt(E) / s), "bq": bf(n(HD) * 0.1),
            "Wk": bf(n((HD, E)) / np.sqrt(E) / s), "bk": bf(n(HD) * 0.1),
            "Wv": bf(n((HD, E)) / np.sqrt(E) / s), "bv": bf(n(HD) * 0.1)}


def reference(input, Wq, bq, Wk, bk, Wv, bv):
    xq = mxq(f64(input), 2, "e4m3")
    q = split_heads(l2norm((xq @ mxq(f64(Wq), 1, "e4m3").T) + f64(bq)))
    k = split_heads(l2norm((xq @ mxq(f64(Wk), 1, "e4m3").T) + f64(bk)))
    v = split_heads((xq @ mxq(f64(Wv), 1, "e4m3").T) + f64(bv))
    return q, k, v

@@ -1,0 +1,196 @@
+from contextlib import ExitStack
+
+import concourse.mybir as mybir
+from concourse.masks import make_identity
+
+FLOPS = 2 * 512 * 1024 * 3072
+
+FP8X4 = mybir.dt.float8_e4m3fn_x4
+F32 = mybir.dt.float32
+BF16 = mybir.dt.bfloat16
+U32 = mybir.dt.uint32
+U8 = mybir.dt.uint8
+I32 = mybir.dt.int32
+ALU = mybir.AluOpType
+ACT = mybir.ActivationFunctionType
+
+P = 128
+E = 1024
+NBLK = 512
+
+VEC_E = {0: (1, 3), 1: (1, 3), 2: (), 3: (), 4: (), 5: (), 6: ()}
+
+
+def tile_knnxlmultiheadsattention_pa_kernel(
+    tc, x_in, wq, bq, wk, bk, wv, bv, out_q, out_k, out_v
+):
+    nc = tc.nc
+    weights = (wq, wk, wv)
+    biases = (bq, bk, bv)
+    outs = (out_q, out_k, out_v)
+    with ExitStack() as ctx:
+        const = ctx.enter_context(tc.tile_pool(name="const", bufs=1))
+        raw = ctx.enter_context(tc.tile_pool(name="raw", bufs=1))
+        grp = ctx.enter_context(tc.tile_pool(name="grp", bufs=3))
+        keep = ctx.enter_context(tc.tile_pool(name="keep", bufs=1))
+        res = ctx.enter_context(tc.tile_pool(name="res", bufs=1))
+        scr = ctx.enter_context(tc.tile_pool(name="scr", bufs=2))
+        small = ctx.enter_context(tc.tile_pool(name="small", bufs=1))
+        tpp = ctx.enter_context(tc.psum_pool(name="tpp", bufs=4))
+        accp = ctx.enter_context(tc.psum_pool(name="accp", bufs=4))
+
+        bzs = []
+        for w in range(3):
+            bz = const.tile([P, E], BF16, name="bz%d" % w)
+            nc.vector.memset(bz[:].bitcast(I32), 0)
+            nc.scalar.dma_start(out=bz[0:1, :], in_=biases[w].rearrange("(o n) -> o n", o=1))
+            bzs.append(bz)
+
+        rows = []
+        xr = []
+        for b in range(2):
+            t = raw.tile([P, 2, E], BF16, name="xraw%d" % b)
+            nc.sync.dma_start(out=t[:], in_=x_in[b].rearrange("(p j) e -> p j e", j=2))
+            xr.extend([t[:, 0, :], t[:, 1, :]])
+        rows.append(xr)
+        for w in range(3):
+            for c in range(2):
+                wsrc = weights[w][c * NBLK : (c + 1) * NBLK, :].rearrange("(p r) k -> p r k", r=4)
+                wr = []
+                for hf in range(2):
+                    t = raw.tile([P, 2, E], BF16, name="wraw%d%d%d" % (w, c, hf))
+                    nc.sync.dma_start(out=t[:], in_=wsrc[:, 2 * hf : 2 * hf + 2, :])
+                    wr.extend([t[:, 0, :], t[:, 1, :]])
+                rows.append(wr)
+
+        ident = const.tile([P, P], F32, name="ident")
+        make_identity(nc, ident[:])
+        ones = const.tile([P, P], BF16, name="ones")
+        nc.gpsimd.memset(ones[:], 1.0)
+        one1 = small.tile([P, 1], F32, name="one1")
+        nc.vector.memset(one1[:], 1.0)
+        one2 = small.tile([P, 1], F32, name="one2")
+        nc.scalar.activation(out=one2[:], in_=one1[:], func=ACT.Sqrt)
+
+        bias = []
+
+        def spread_biases():
+            for w in range(3):
+                pb = accp.tile([P, E], BF16, tag="acc", name="pb%d" % w)
+                for c in range(2):
+                    nc.tensor.matmul(
+                        out=pb[:, c * NBLK : (c + 1) * NBLK],
+                        lhsT=ones[:],
+                        rhs=bzs[w][:, c * NBLK : (c + 1) * NBLK],
+                        start=True,
+                        stop=True,
+                    )
+                bb = const.tile([P, E], BF16, name="bias%d" % w)
+                if w == 1:
+                    nc.vector.tensor_copy(out=bb[:], in_=pb[:])
+                else:
+                    nc.scalar.copy(out=bb[:], in_=pb[:])
+                bias.append(bb)
+
+        codes = []
+        planes = []
+
+        def prepare(blk):
+            g4 = grp.tile([P, 2, NBLK, 4], BF16, tag="g4", name="g4_%d" % blk, align_bytes=64)
+            gw = g4[:].bitcast(F32)
+            for r in range(4):
+                tp = tpp.tile([P, 2, 2, P], F32, tag="tp", name="tp%d_%d" % (blk, r))
+                src = rows[blk][r].bitcast(F32)
+                for g in range(2):
+                    for u in range(2):
+                        k0 = 256 * g + 128 * u
+                        nc.tensor.transpose(tp[:, g, u, :], src[:, k0 : k0 + P], ident[:])
+                dst = gw[:, :, r * P : (r + 1) * P, :]
+                view = tp[:].rearrange("p g u r -> p g r u")
+                if r in VEC_E[blk]:
+                    nc.vector.tensor_copy(out=dst, in_=view)
+                else:
+                    nc.scalar.copy(out=dst, in_=view)
+            cd = keep.tile([P, 2, NBLK], U32, name="cd%d" % blk, align_bytes=64)
+            pl = keep.tile([P, 2, NBLK], U8, name="pl%d" % blk, align_bytes=64)
+            for g in range(2):
+                nc.vector.quantize_mx(
+                    out=cd[:, g, :].bitcast(FP8X4),
+                    scales=pl[:, g, :],
+                    in_=g4[:, g, :, :].rearrange("p f t -> p (f t)"),
+                )
+            codes.append(cd)
+            planes.append(pl)
+
+        result = {}
+        sumsq = {}
+
+        def multiply(blk):
+            w, c = divmod(blk - 1, 2)
+            if c == 0:
+                for b in range(2):
+                    result[(w, b)] = res.tile([P, 8, 2, P], F32, name="o%d%d" % (w, b))
+                if w < 2:
+                    sumsq[w] = small.tile([P, 2, 4], F32, name="ss%d" % w)
+            for tt in range(4):
+                b, jj = divmod(tt, 2)
+                acc = accp.tile([P, NBLK], F32, tag="acc", name="acc%d_%d" % (blk, tt))
+                for g in range(2):
+                    nc.tensor.matmul_mx(
+                        out=acc[:],
+                        lhsT=codes[0][:, g, tt * P : (tt + 1) * P].bitcast(FP8X4),
+                        lhsT_scale=planes[0][:, g, tt * P : (tt + 1) * P],
+                        rhs=codes[blk][:, g, :].bitcast(FP8X4),
+                        rhs_scale=planes[blk][:, g, :],
+                        start=(g == 0),
+                        stop=(g == 1),
+                    )
+                y = result[(w, b)][:, 4 * c : 4 * c + 4, jj, :]
+                nc.vector.tensor_tensor(
+                    out=y.rearrange("p h (e r) -> p h e r", r=4),
+                    in0=acc[:].rearrange("p (r h e) -> p h e r", r=4, h=4),
+                    in1=bias[w][:, c * NBLK : (c + 1) * NBLK].rearrange("p (h e r) -> p h e r", h=4, r=4),
+                    op=ALU.add,
+                )
+                if w < 2:
+                    junk = scr.tile([P, 4, P], F32, tag="junk", name="junk%d_%d" % (blk, tt))
+                    nc.scalar.activation(
+                        out=junk[:], in_=y, func=ACT.Square, accum_out=sumsq[w][:, c, tt : tt + 1]
+                    )
+                elif jj == 1:
+                    nc.sync.dma_start(
+                        out=outs[w][b, 4 * c : 4 * c + 4].rearrange("h (p j) d -> p h (j d)", j=2),
+                        in_=result[(w, b)][:, 4 * c : 4 * c + 4, :, :].rearrange("p h j d -> p h (j d)"),
+                    )
+
+        def normalise(w):
+            s4 = small.tile([P, 4], F32, name="s4_%d" % w)
+            nc.vector.tensor_tensor(out=s4[:], in0=sumsq[w][:, 0, :], in1=sumsq[w][:, 1, :], op=ALU.add)
+            m4 = small.tile([P, 4], F32, name="m4_%d" % w)
+            nc.vector.tensor_scalar(out=m4[:], in0=s4[:], scalar1=1e-24, scalar2=None, op0=ALU.max)
+            n4 = small.tile([P, 4], F32, name="n4_%d" % w)
+            nc.scalar.activation(out=n4[:], in_=m4[:], func=ACT.Sqrt)
+            r4 = small.tile([P, 4], F32, name="r4_%d" % w)
+            nc.vector.reciprocal(out=r4[:], in_=n4[:])
+            for tt in range(4):
+                b, jj = divmod(tt, 2)
+                y = result[(w, b)][:, :, jj, :]
+                nc.vector.tensor_scalar(
+                    out=y, in0=y, scalar1=r4[:, tt : tt + 1], scalar2=None, op0=ALU.mult
+                )
+                if jj == 1:
+                    nc.sync.dma_start(
+                        out=outs[w][b].rearrange("h (p j) d -> p h (j d)", j=2),
+                        in_=result[(w, b)][:].rearrange("p h j d -> p h (j d)"),
+                    )
+
+        prepare(0)
+        prepare(1)
+        spread_biases()
+        prepare(2)
+        for blk in range(1, 7):
+            multiply(blk)
+            if blk in (2, 4):
+                normalise(blk // 2 - 1)
+            if blk + 2 < 7:
+                prepare(blk + 2)

@@ -18,7 +18,19 @@ P = 128
 E = 1024
 NBLK = 512
 
-VEC_E = {0: (1, 3), 1: (1, 3), 2: (), 3: (), 4: (), 5: (), 6: ()}
+VEC_E = {0: (1, 3), 1: (1, 3), 2: (3,), 3: (3,), 4: (3,), 5: (3,), 6: (3,)}
+R_ENG = ("V", "S")
+TRUN = 2
+LEAD_T = 1.0
+LEAD_E = 0.0
+DQ = 0.5
+DS = 0.5
+DN = 1.5
+DN4 = 1.0
+DR = 0.1
+KB = (-93.5, -91.5, -89.5)
+BC_ENG = ("S", "V", "S")
+BUFS = {"tp": 4, "acc": 4, "grp": 3}
 
 
 def tile_knnxlmultiheadsattention_pa_kernel(
@@ -29,15 +41,16 @@ def tile_knnxlmultiheadsattention_pa_kernel(
     biases = (bq, bk, bv)
     outs = (out_q, out_k, out_v)
     with ExitStack() as ctx:
+        ctx.enter_context(tc.manual_schedule())
         const = ctx.enter_context(tc.tile_pool(name="const", bufs=1))
         raw = ctx.enter_context(tc.tile_pool(name="raw", bufs=1))
-        grp = ctx.enter_context(tc.tile_pool(name="grp", bufs=3))
+        grp = ctx.enter_context(tc.tile_pool(name="grp", bufs=BUFS["grp"]))
         keep = ctx.enter_context(tc.tile_pool(name="keep", bufs=1))
         res = ctx.enter_context(tc.tile_pool(name="res", bufs=1))
         scr = ctx.enter_context(tc.tile_pool(name="scr", bufs=2))
         small = ctx.enter_context(tc.tile_pool(name="small", bufs=1))
-        tpp = ctx.enter_context(tc.psum_pool(name="tpp", bufs=4))
-        accp = ctx.enter_context(tc.psum_pool(name="accp", bufs=4))
+        tpp = ctx.enter_context(tc.psum_pool(name="tpp", bufs=BUFS["tp"]))
+        accp = ctx.enter_context(tc.psum_pool(name="accp", bufs=BUFS["acc"]))
 
         bzs = []
         for w in range(3):
@@ -72,125 +85,240 @@ def tile_knnxlmultiheadsattention_pa_kernel(
         one2 = small.tile([P, 1], F32, name="one2")
         nc.scalar.activation(out=one2[:], in_=one1[:], func=ACT.Sqrt)
 
-        bias = []
+        ops = {}
+        queues = {"PE": [], "V": [], "S": [], "SP": []}
 
-        def spread_biases():
-            for w in range(3):
-                pb = accp.tile([P, E], BF16, tag="acc", name="pb%d" % w)
-                for c in range(2):
-                    nc.tensor.matmul(
-                        out=pb[:, c * NBLK : (c + 1) * NBLK],
-                        lhsT=ones[:],
-                        rhs=bzs[w][:, c * NBLK : (c + 1) * NBLK],
-                        start=True,
-                        stop=True,
-                    )
-                bb = const.tile([P, E], BF16, name="bias%d" % w)
-                if w == 1:
-                    nc.vector.tensor_copy(out=bb[:], in_=pb[:])
-                else:
-                    nc.scalar.copy(out=bb[:], in_=pb[:])
-                bias.append(bb)
+        def add(eng, key, name, deps, emit, takes=(), frees=()):
+            ops[name] = (deps, emit, takes, frees)
+            queues[eng].append((key, len(ops), name))
 
-        codes = []
-        planes = []
+        tiles = {}
 
-        def prepare(blk):
-            g4 = grp.tile([P, 2, NBLK, 4], BF16, tag="g4", name="g4_%d" % blk, align_bytes=64)
-            gw = g4[:].bitcast(F32)
-            for r in range(4):
-                tp = tpp.tile([P, 2, 2, P], F32, tag="tp", name="tp%d_%d" % (blk, r))
-                src = rows[blk][r].bitcast(F32)
-                for g in range(2):
-                    for u in range(2):
-                        k0 = 256 * g + 128 * u
-                        nc.tensor.transpose(tp[:, g, u, :], src[:, k0 : k0 + P], ident[:])
-                dst = gw[:, :, r * P : (r + 1) * P, :]
-                view = tp[:].rearrange("p g u r -> p g r u")
-                if r in VEC_E[blk]:
-                    nc.vector.tensor_copy(out=dst, in_=view)
-                else:
-                    nc.scalar.copy(out=dst, in_=view)
-            cd = keep.tile([P, 2, NBLK], U32, name="cd%d" % blk, align_bytes=64)
-            pl = keep.tile([P, 2, NBLK], U8, name="pl%d" % blk, align_bytes=64)
+        def copy_on(eng, out, in_):
+            if eng == "V":
+                nc.vector.tensor_copy(out=out, in_=in_)
+            else:
+                nc.scalar.copy(out=out, in_=in_)
+
+        def emit_bmm(w):
+            pb = accp.tile([P, E], BF16, tag="acc", name="pb%d" % w)
+            tiles[("pb", w)] = pb
+            for c in range(2):
+                nc.tensor.matmul(
+                    out=pb[:, c * NBLK : (c + 1) * NBLK],
+                    lhsT=ones[:],
+                    rhs=bzs[w][:, c * NBLK : (c + 1) * NBLK],
+                    start=True,
+                    stop=True,
+                )
+
+        def emit_bc(w):
+            bb = const.tile([P, E], BF16, name="bias%d" % w)
+            tiles[("bias", w)] = bb
+            copy_on(BC_ENG[w], bb[:], tiles[("pb", w)][:])
+
+        for w in range(3):
+            add("PE", KB[w], "bmm%d" % w, (), lambda w=w: emit_bmm(w), takes=("acc",))
+            add(BC_ENG[w], KB[w] + 0.3, "bc%d" % w, ("bmm%d" % w,), lambda w=w: emit_bc(w), frees=("acc",))
+
+        def emit_t(blk, r):
+            if r == 0:
+                tiles[("g4", blk)] = grp.tile(
+                    [P, 2, NBLK, 4], BF16, tag="g4", name="g4_%d" % blk, align_bytes=64
+                )
+            tp = tpp.tile([P, 2, 2, P], F32, tag="tp", name="tp%d_%d" % (blk, r))
+            tiles[("tp", blk, r)] = tp
+            src = rows[blk][r].bitcast(F32)
             for g in range(2):
-                nc.vector.quantize_mx(
-                    out=cd[:, g, :].bitcast(FP8X4),
-                    scales=pl[:, g, :],
-                    in_=g4[:, g, :, :].rearrange("p f t -> p (f t)"),
+                for u in range(2):
+                    k0 = 256 * g + 128 * u
+                    nc.tensor.transpose(tp[:, g, u, :], src[:, k0 : k0 + P], ident[:])
+
+        def emit_e(blk, r, eng):
+            gw = tiles[("g4", blk)][:].bitcast(F32)
+            copy_on(
+                eng,
+                gw[:, :, r * P : (r + 1) * P, :],
+                tiles[("tp", blk, r)][:].rearrange("p g u r -> p g r u"),
+            )
+
+        def emit_q(blk, g):
+            if g == 0:
+                tiles[("cd", blk)] = keep.tile([P, 2, NBLK], U32, name="cd%d" % blk, align_bytes=64)
+                tiles[("pl", blk)] = keep.tile([P, 2, NBLK], U8, name="pl%d" % blk, align_bytes=64)
+            nc.vector.quantize_mx(
+                out=tiles[("cd", blk)][:, g, :].bitcast(FP8X4),
+                scales=tiles[("pl", blk)][:, g, :],
+                in_=tiles[("g4", blk)][:, g, :, :].rearrange("p f t -> p (f t)"),
+            )
+
+        for blk in range(7):
+            for r in range(4):
+                if blk <= 2:
+                    kt = -100.0 + 4 * blk + r
+                    ke = kt
+                else:
+                    j = 4 * (blk - 3) + r
+                    kt = TRUN * (j // TRUN) - LEAD_T + 0.01 * j - 0.5
+                    ke = j - LEAD_E
+                eng = "V" if r in VEC_E[blk] else "S"
+                add(
+                    "PE", kt, "T%d.%d" % (blk, r), (), lambda blk=blk, r=r: emit_t(blk, r),
+                    takes=("tp", "grp") if r == 0 else ("tp",),
                 )
-            codes.append(cd)
-            planes.append(pl)
+                add(
+                    eng, ke + 0.001, "E%d.%d" % (blk, r), ("T%d.%d" % (blk, r),),
+                    lambda blk=blk, r=r, eng=eng: emit_e(blk, r, eng), frees=("tp",),
+                )
+            for g in range(2):
+                if blk <= 2:
+                    kq = -100.0 + 4 * blk + 3.5 + 0.1 * g
+                else:
+                    kq = 4 * (blk - 3) + 3 - LEAD_E + DQ + 0.1 * g
+                add(
+                    "V", kq, "Q%d.%d" % (blk, g), tuple("E%d.%d" % (blk, r) for r in range(4)),
+                    lambda blk=blk, g=g: emit_q(blk, g), frees=("grp",) if g == 1 else (),
+                )
 
-        result = {}
-        sumsq = {}
+        def emit_m(blk, tt):
+            acc = accp.tile([P, NBLK], F32, tag="acc", name="acc%d_%d" % (blk, tt))
+            tiles[("acc", blk, tt)] = acc
+            for g in range(2):
+                nc.tensor.matmul_mx(
+                    out=acc[:],
+                    lhsT=tiles[("cd", 0)][:, g, tt * P : (tt + 1) * P].bitcast(FP8X4),
+                    lhsT_scale=tiles[("pl", 0)][:, g, tt * P : (tt + 1) * P],
+                    rhs=tiles[("cd", blk)][:, g, :].bitcast(FP8X4),
+                    rhs_scale=tiles[("pl", blk)][:, g, :],
+                    start=(g == 0),
+                    stop=(g == 1),
+                )
 
-        def multiply(blk):
+        def emit_a(blk, tt):
             w, c = divmod(blk - 1, 2)
-            if c == 0:
-                for b in range(2):
-                    result[(w, b)] = res.tile([P, 8, 2, P], F32, name="o%d%d" % (w, b))
-                if w < 2:
-                    sumsq[w] = small.tile([P, 2, 4], F32, name="ss%d" % w)
-            for tt in range(4):
-                b, jj = divmod(tt, 2)
-                acc = accp.tile([P, NBLK], F32, tag="acc", name="acc%d_%d" % (blk, tt))
-                for g in range(2):
-                    nc.tensor.matmul_mx(
-                        out=acc[:],
-                        lhsT=codes[0][:, g, tt * P : (tt + 1) * P].bitcast(FP8X4),
-                        lhsT_scale=planes[0][:, g, tt * P : (tt + 1) * P],
-                        rhs=codes[blk][:, g, :].bitcast(FP8X4),
-                        rhs_scale=planes[blk][:, g, :],
-                        start=(g == 0),
-                        stop=(g == 1),
-                    )
-                y = result[(w, b)][:, 4 * c : 4 * c + 4, jj, :]
-                nc.vector.tensor_tensor(
-                    out=y.rearrange("p h (e r) -> p h e r", r=4),
-                    in0=acc[:].rearrange("p (r h e) -> p h e r", r=4, h=4),
-                    in1=bias[w][:, c * NBLK : (c + 1) * NBLK].rearrange("p (h e r) -> p h e r", h=4, r=4),
-                    op=ALU.add,
-                )
-                if w < 2:
-                    junk = scr.tile([P, 4, P], F32, tag="junk", name="junk%d_%d" % (blk, tt))
-                    nc.scalar.activation(
-                        out=junk[:], in_=y, func=ACT.Square, accum_out=sumsq[w][:, c, tt : tt + 1]
-                    )
-                elif jj == 1:
-                    nc.sync.dma_start(
-                        out=outs[w][b, 4 * c : 4 * c + 4].rearrange("h (p j) d -> p h (j d)", j=2),
-                        in_=result[(w, b)][:, 4 * c : 4 * c + 4, :, :].rearrange("p h j d -> p h (j d)"),
-                    )
+            b, jj = divmod(tt, 2)
+            if (w, b) not in tiles:
+                tiles[(w, b)] = res.tile([P, 8, 2, P], F32, name="o%d%d" % (w, b))
+            y = tiles[(w, b)][:, 4 * c : 4 * c + 4, jj, :]
+            nc.vector.tensor_tensor(
+                out=y.rearrange("p h (e r) -> p h e r", r=4),
+                in0=tiles[("acc", blk, tt)][:].rearrange("p (r h e) -> p h e r", r=4, h=4),
+                in1=tiles[("bias", w)][:, c * NBLK : (c + 1) * NBLK].rearrange(
+                    "p (h e r) -> p h e r", h=4, r=4
+                ),
+                op=ALU.add,
+            )
 
-        def normalise(w):
-            s4 = small.tile([P, 4], F32, name="s4_%d" % w)
-            nc.vector.tensor_tensor(out=s4[:], in0=sumsq[w][:, 0, :], in1=sumsq[w][:, 1, :], op=ALU.add)
-            m4 = small.tile([P, 4], F32, name="m4_%d" % w)
-            nc.vector.tensor_scalar(out=m4[:], in0=s4[:], scalar1=1e-24, scalar2=None, op0=ALU.max)
-            n4 = small.tile([P, 4], F32, name="n4_%d" % w)
-            nc.scalar.activation(out=n4[:], in_=m4[:], func=ACT.Sqrt)
-            r4 = small.tile([P, 4], F32, name="r4_%d" % w)
-            nc.vector.reciprocal(out=r4[:], in_=n4[:])
-            for tt in range(4):
-                b, jj = divmod(tt, 2)
-                y = result[(w, b)][:, :, jj, :]
+        def emit_sq(w, tt):
+            b, jj = divmod(tt, 2)
+            if ("ss", w) not in tiles:
+                tiles[("ss", w)] = small.tile([P, 4], F32, name="ss%d" % w)
+            junk = scr.tile([P, 8, P], F32, tag="junk", name="junk%d_%d" % (w, tt))
+            nc.scalar.activation(
+                out=junk[:], in_=tiles[(w, b)][:, :, jj, :], func=ACT.Square,
+                accum_out=tiles[("ss", w)][:, tt : tt + 1],
+            )
+
+        def emit_n(step, w, b):
+            if step == 2:
+                m2 = small.tile([P, 2], F32, name="m2_%d%d" % (w, b))
+                tiles[("m2", w, b)] = m2
                 nc.vector.tensor_scalar(
-                    out=y, in0=y, scalar1=r4[:, tt : tt + 1], scalar2=None, op0=ALU.mult
+                    out=m2[:], in0=tiles[("ss", w)][:, 2 * b : 2 * b + 2], scalar1=1e-24, scalar2=None,
+                    op0=ALU.max,
                 )
-                if jj == 1:
-                    nc.sync.dma_start(
-                        out=outs[w][b].rearrange("h (p j) d -> p h (j d)", j=2),
-                        in_=result[(w, b)][:].rearrange("p h j d -> p h (j d)"),
-                    )
+            elif step == 3:
+                n2 = small.tile([P, 2], F32, name="n2_%d%d" % (w, b))
+                tiles[("n2", w, b)] = n2
+                nc.scalar.activation(out=n2[:], in_=tiles[("m2", w, b)][:], func=ACT.Sqrt)
+            else:
+                r2 = small.tile([P, 2], F32, name="r2_%d%d" % (w, b))
+                tiles[("r2", w, b)] = r2
+                nc.vector.reciprocal(out=r2[:], in_=tiles[("n2", w, b)][:])
 
-        prepare(0)
-        prepare(1)
-        spread_biases()
-        prepare(2)
-        for blk in range(1, 7):
-            multiply(blk)
-            if blk in (2, 4):
-                normalise(blk // 2 - 1)
-            if blk + 2 < 7:
-                prepare(blk + 2)
+        def emit_r(w, tt, eng):
+            b, jj = divmod(tt, 2)
+            y = tiles[(w, b)][:, :, jj, :]
+            rr = tiles[("r2", w, b)][:, jj : jj + 1]
+            if eng == "V":
+                nc.vector.tensor_scalar(out=y, in0=y, scalar1=rr, scalar2=None, op0=ALU.mult)
+            else:
+                nc.scalar.activation(out=y, in_=y, func=ACT.Copy, scale=rr)
+
+        def emit_store(w, b, h0, h1):
+            nc.sync.dma_start(
+                out=outs[w][b, h0:h1].rearrange("h (p j) d -> p h (j d)", j=2),
+                in_=tiles[(w, b)][:, h0:h1, :, :].rearrange("p h j d -> p h (j d)"),
+            )
+
+        units = [
+            (2 * w + 1 + c, 2 * b + jj)
+            for w in range(3) for b in range(2) for c in range(2) for jj in range(2)
+        ]
+        slot = {}
+        for i, (blk, tt) in enumerate(units):
+            slot[(blk, tt)] = i
+            w = (blk - 1) // 2
+            add(
+                "PE", float(i), "M%d.%d" % (blk, tt), ("Q0.0", "Q0.1", "Q%d.0" % blk, "Q%d.1" % blk),
+                lambda blk=blk, tt=tt: emit_m(blk, tt), takes=("acc",),
+            )
+            add(
+                "V", i + 0.2, "A%d.%d" % (blk, tt), ("M%d.%d" % (blk, tt), "bc%d" % w),
+                lambda blk=blk, tt=tt: emit_a(blk, tt), frees=("acc",),
+            )
+        for w in range(2):
+            for b in range(2):
+                last = 0
+                for tt in (2 * b, 2 * b + 1):
+                    j = max(slot[(2 * w + 1, tt)], slot[(2 * w + 2, tt)])
+                    last = max(last, j)
+                    add(
+                        "S", j + DS, "Sq%d.%d" % (w, tt), ("A%d.%d" % (2 * w + 1, tt), "A%d.%d" % (2 * w + 2, tt)),
+                        lambda w=w, tt=tt: emit_sq(w, tt),
+                    )
+                t = "%d%d" % (w, b)
+                add("V", last + DN, "N2." + t, ("Sq%d.%d" % (w, 2 * b), "Sq%d.%d" % (w, 2 * b + 1)),
+                    lambda w=w, b=b: emit_n(2, w, b))
+                add("S", last + DN + 0.05, "N3." + t, ("N2." + t,), lambda w=w, b=b: emit_n(3, w, b))
+                add("V", last + DN + DN4, "N4." + t, ("N3." + t,), lambda w=w, b=b: emit_n(4, w, b))
+                for q, tt in enumerate((2 * b, 2 * b + 1)):
+                    add(
+                        R_ENG[q], last + DN + DN4 + 0.01 + q * DR, "R%d.%d" % (w, tt), ("N4." + t,),
+                        lambda w=w, tt=tt, q=q: emit_r(w, tt, R_ENG[q]),
+                    )
+                add("SP", last + 3.0, "St" + t, ("R%d.%d" % (w, 2 * b), "R%d.%d" % (w, 2 * b + 1)),
+                    lambda w=w, b=b: emit_store(w, b, 0, 8))
+        for c in range(2):
+            for b in range(2):
+                add(
+                    "SP", float(slot[(5 + c, 2 * b + 1)]), "Stv%d%d" % (c, b),
+                    ("A%d.%d" % (5 + c, 2 * b), "A%d.%d" % (5 + c, 2 * b + 1)),
+                    lambda c=c, b=b: emit_store(2, b, 4 * c, 4 * c + 4),
+                )
+
+        order = {e: [n for (k, i, n) in sorted(q)] for e, q in queues.items()}
+        head = {e: 0 for e in order}
+        done = set()
+        held = {"tp": 0, "acc": 0, "grp": 0}
+        left = len(ops)
+        while left:
+            moved = False
+            for e in ("PE", "S", "V", "SP"):
+                while head[e] < len(order[e]):
+                    name = order[e][head[e]]
+                    deps, emit, takes, frees = ops[name]
+                    if not all(d in done for d in deps):
+                        break
+                    if not all(held[p] < BUFS[p] for p in takes):
+                        break
+                    emit()
+                    for p in takes:
+                        held[p] += 1
+                    for p in frees:
+                        held[p] -= 1
+                    done.add(name)
+                    head[e] += 1
+                    left -= 1
+                    moved = True
+            assert moved, "the orders of the engines block each other"

@@ -19,13 +19,13 @@ E = 1024
 NBLK = 512
 
 VEC_E = {0: (1, 3), 1: (1, 3), 2: (3,), 3: (3,), 4: (3,), 5: (3,), 6: (3,)}
-R_ENG = ("V", "S")
+R_ENG = {(0, 0): "G", (0, 1): "G", (1, 0): "S", (1, 1): "G"}
 TRUN = 2
 LEAD_T = 1.0
 LEAD_E = 0.0
 DQ = 0.5
-DS = 0.5
-DN = 1.5
+DS = 1.5
+DN = 2.5
 DN4 = 1.0
 DR = 0.1
 KB = (-93.5, -91.5, -89.5)
@@ -86,7 +86,7 @@ def tile_knnxlmultiheadsattention_pa_kernel(
         nc.scalar.activation(out=one2[:], in_=one1[:], func=ACT.Sqrt)
 
         ops = {}
-        queues = {"PE": [], "V": [], "S": [], "SP": []}
+        queues = {"PE": [], "V": [], "S": [], "G": [], "SP": []}
 
         def add(eng, key, name, deps, emit, takes=(), frees=()):
             ops[name] = (deps, emit, takes, frees)
@@ -242,6 +242,8 @@ def tile_knnxlmultiheadsattention_pa_kernel(
             rr = tiles[("r2", w, b)][:, jj : jj + 1]
             if eng == "V":
                 nc.vector.tensor_scalar(out=y, in0=y, scalar1=rr, scalar2=None, op0=ALU.mult)
+            elif eng == "G":
+                nc.gpsimd.tensor_scalar(out=y, in0=y, scalar1=rr, scalar2=1.0, op0=ALU.mult, op1=ALU.mult)
             else:
                 nc.scalar.activation(out=y, in_=y, func=ACT.Copy, scale=rr)
 
@@ -284,8 +286,8 @@ def tile_knnxlmultiheadsattention_pa_kernel(
                 add("V", last + DN + DN4, "N4." + t, ("N3." + t,), lambda w=w, b=b: emit_n(4, w, b))
                 for q, tt in enumerate((2 * b, 2 * b + 1)):
                     add(
-                        R_ENG[q], last + DN + DN4 + 0.01 + q * DR, "R%d.%d" % (w, tt), ("N4." + t,),
-                        lambda w=w, tt=tt, q=q: emit_r(w, tt, R_ENG[q]),
+                        R_ENG[(w, q)], last + DN + DN4 + 0.01 + q * DR, "R%d.%d" % (w, tt), ("N4." + t,),
+                        lambda w=w, tt=tt, q=q: emit_r(w, tt, R_ENG[(w, q)]),
                     )
                 add("SP", last + 3.0, "St" + t, ("R%d.%d" % (w, 2 * b), "R%d.%d" % (w, 2 * b + 1)),
                     lambda w=w, b=b: emit_store(w, b, 0, 8))
@@ -304,7 +306,7 @@ def tile_knnxlmultiheadsattention_pa_kernel(
         left = len(ops)
         while left:
             moved = False
-            for e in ("PE", "S", "V", "SP"):
+            for e in ("PE", "S", "V", "G", "SP"):
                 while head[e] < len(order[e]):
                     name = order[e][head[e]]
                     deps, emit, takes, frees = ops[name]

@@ -19,13 +19,13 @@ E = 1024
 NBLK = 512
 
 VEC_E = {0: (1, 3), 1: (1, 3), 2: (3,), 3: (3,), 4: (3,), 5: (3,), 6: (3,)}
-R_ENG = {(0, 0): "G", (0, 1): "G", (1, 0): "S", (1, 1): "G"}
+R_ENG = ("V", "S")
 TRUN = 2
 LEAD_T = 1.0
 LEAD_E = 0.0
 DQ = 0.5
-DS = 1.5
-DN = 2.5
+DS = 0.5
+DN = 1.5
 DN4 = 1.0
 DR = 0.1
 KB = (-93.5, -91.5, -89.5)
@@ -86,7 +86,7 @@ def tile_knnxlmultiheadsattention_pa_kernel(
         nc.scalar.activation(out=one2[:], in_=one1[:], func=ACT.Sqrt)
 
         ops = {}
-        queues = {"PE": [], "V": [], "S": [], "G": [], "SP": []}
+        queues = {"PE": [], "V": [], "S": [], "SP": []}
 
         def add(eng, key, name, deps, emit, takes=(), frees=()):
             ops[name] = (deps, emit, takes, frees)
@@ -242,8 +242,6 @@ def tile_knnxlmultiheadsattention_pa_kernel(
             rr = tiles[("r2", w, b)][:, jj : jj + 1]
             if eng == "V":
                 nc.vector.tensor_scalar(out=y, in0=y, scalar1=rr, scalar2=None, op0=ALU.mult)
-            elif eng == "G":
-                nc.gpsimd.tensor_scalar(out=y, in0=y, scalar1=rr, scalar2=1.0, op0=ALU.mult, op1=ALU.mult)
             else:
                 nc.scalar.activation(out=y, in_=y, func=ACT.Copy, scale=rr)
 
@@ -286,11 +284,12 @@ def tile_knnxlmultiheadsattention_pa_kernel(
                 add("V", last + DN + DN4, "N4." + t, ("N3." + t,), lambda w=w, b=b: emit_n(4, w, b))
                 for q, tt in enumerate((2 * b, 2 * b + 1)):
                     add(
-                        R_ENG[(w, q)], last + DN + DN4 + 0.01 + q * DR, "R%d.%d" % (w, tt), ("N4." + t,),
-                        lambda w=w, tt=tt, q=q: emit_r(w, tt, R_ENG[(w, q)]),
+                        R_ENG[q], last + DN + DN4 + 0.01 + q * DR, "R%d.%d" % (w, tt), ("N4." + t,),
+                        lambda w=w, tt=tt, q=q: emit_r(w, tt, R_ENG[q]),
                     )
-                add("SP", last + 3.0, "St" + t, ("R%d.%d" % (w, 2 * b), "R%d.%d" % (w, 2 * b + 1)),
-                    lambda w=w, b=b: emit_store(w, b, 0, 8))
+                for c in range(2):
+                    add("SP", last + 3.0 + 0.1 * c, "St%s%d" % (t, c), ("R%d.%d" % (w, 2 * b), "R%d.%d" % (w, 2 * b + 1)),
+                        lambda w=w, b=b, c=c: emit_store(w, b, 4 * c, 4 * c + 4))
         for c in range(2):
             for b in range(2):
                 add(
@@ -306,7 +305,7 @@ def tile_knnxlmultiheadsattention_pa_kernel(
         left = len(ops)
         while left:
             moved = False
-            for e in ("PE", "S", "V", "G", "SP"):
+            for e in ("PE", "S", "V", "SP"):
                 while head[e] < len(order[e]):
                     name = order[e][head[e]]
                     deps, emit, takes, frees = ops[name]

@@ -28,7 +28,8 @@ DS = 0.5
 DN = 1.5
 DN4 = 1.0
 DR = 0.1
-KB = (-93.5, -91.5, -89.5)
+KB = (-94.5, -92.5, -90.5)
+WARM = ((-101.0, 4), (-98.5, 2), (-96.5, 2))
 BC_ENG = ("S", "V", "S")
 BUFS = {"tp": 4, "acc": 4, "grp": 3}
 
@@ -51,6 +52,11 @@ def tile_knnxlmultiheadsattention_pa_kernel(
         small = ctx.enter_context(tc.tile_pool(name="small", bufs=1))
         tpp = ctx.enter_context(tc.psum_pool(name="tpp", bufs=BUFS["tp"]))
         accp = ctx.enter_context(tc.psum_pool(name="accp", bufs=BUFS["acc"]))
+
+        ones = const.tile([P, P], BF16, name="ones")
+        nc.gpsimd.memset(ones[:], 1.0)
+        dz = const.tile([P, NBLK], BF16, name="dz")
+        nc.vector.memset(dz[:].bitcast(I32), 0)
 
         bzs = []
         for w in range(3):
@@ -78,8 +84,6 @@ def tile_knnxlmultiheadsattention_pa_kernel(
 
         ident = const.tile([P, P], F32, name="ident")
         make_identity(nc, ident[:])
-        ones = const.tile([P, P], BF16, name="ones")
-        nc.gpsimd.memset(ones[:], 1.0)
         one1 = small.tile([P, 1], F32, name="one1")
         nc.vector.memset(one1[:], 1.0)
         one2 = small.tile([P, 1], F32, name="one2")
@@ -116,6 +120,14 @@ def tile_knnxlmultiheadsattention_pa_kernel(
             bb = const.tile([P, E], BF16, name="bias%d" % w)
             tiles[("bias", w)] = bb
             copy_on(BC_ENG[w], bb[:], tiles[("pb", w)][:])
+
+        def emit_warm(i, n):
+            pd = accp.tile([P, NBLK], F32, tag="acc", name="warm%d" % i)
+            for k in range(n):
+                nc.tensor.matmul(out=pd[:], lhsT=ones[:], rhs=dz[:], start=True, stop=True)
+
+        for i, (key, n) in enumerate(WARM):
+            add("PE", key, "D%d" % i, (), lambda i=i, n=n: emit_warm(i, n), takes=("acc",), frees=("acc",))
 
         for w in range(3):
             add("PE", KB[w], "bmm%d" % w, (), lambda w=w: emit_bmm(w), takes=("acc",))

from contextlib import ExitStack

import concourse.mybir as mybir
from concourse.masks import make_identity

FLOPS = 2 * 512 * 1024 * 3072

FP8X4 = mybir.dt.float8_e4m3fn_x4
F32 = mybir.dt.float32
BF16 = mybir.dt.bfloat16
U32 = mybir.dt.uint32
U8 = mybir.dt.uint8
I32 = mybir.dt.int32
ALU = mybir.AluOpType
ACT = mybir.ActivationFunctionType

P = 128
E = 1024
NBLK = 512

VEC_E = {0: (1, 3), 1: (1, 3), 2: (3,), 3: (3,), 4: (3,), 5: (3,), 6: (3,)}
R_ENG = ("V", "S")
TRUN = 2
LEAD_T = 1.0
LEAD_E = 0.0
DQ = 0.5
DS = 0.5
DN = 1.5
DN4 = 1.0
DR = 0.1
KB = (-94.5, -92.5, -90.5)
WARM = ((-101.0, 4), (-98.5, 2), (-96.5, 2))
BC_ENG = ("S", "V", "S")
BUFS = {"tp": 4, "acc": 4, "grp": 3}


def tile_knnxlmultiheadsattention_pa_kernel(
    tc, x_in, wq, bq, wk, bk, wv, bv, out_q, out_k, out_v
):
    nc = tc.nc
    weights = (wq, wk, wv)
    biases = (bq, bk, bv)
    outs = (out_q, out_k, out_v)
    with ExitStack() as ctx:
        ctx.enter_context(tc.manual_schedule())
        const = ctx.enter_context(tc.tile_pool(name="const", bufs=1))
        raw = ctx.enter_context(tc.tile_pool(name="raw", bufs=1))
        grp = ctx.enter_context(tc.tile_pool(name="grp", bufs=BUFS["grp"]))
        keep = ctx.enter_context(tc.tile_pool(name="keep", bufs=1))
        res = ctx.enter_context(tc.tile_pool(name="res", bufs=1))
        scr = ctx.enter_context(tc.tile_pool(name="scr", bufs=2))
        small = ctx.enter_context(tc.tile_pool(name="small", bufs=1))
        tpp = ctx.enter_context(tc.psum_pool(name="tpp", bufs=BUFS["tp"]))
        accp = ctx.enter_context(tc.psum_pool(name="accp", bufs=BUFS["acc"]))

        ones = const.tile([P, P], BF16, name="ones")
        nc.gpsimd.memset(ones[:], 1.0)
        dz = const.tile([P, NBLK], BF16, name="dz")
        nc.vector.memset(dz[:].bitcast(I32), 0)

        bzs = []
        for w in range(3):
            bz = const.tile([P, E], BF16, name="bz%d" % w)
            nc.vector.memset(bz[:].bitcast(I32), 0)
            nc.scalar.dma_start(out=bz[0:1, :], in_=biases[w].rearrange("(o n) -> o n", o=1))
            bzs.append(bz)

        rows = []
        xr = []
        for b in range(2):
            t = raw.tile([P, 2, E], BF16, name="xraw%d" % b)
            nc.sync.dma_start(out=t[:], in_=x_in[b].rearrange("(p j) e -> p j e", j=2))
            xr.extend([t[:, 0, :], t[:, 1, :]])
        rows.append(xr)
        for w in range(3):
            for c in range(2):
                wsrc = weights[w][c * NBLK : (c + 1) * NBLK, :].rearrange("(p r) k -> p r k", r=4)
                wr = []
                for hf in range(2):
                    t = raw.tile([P, 2, E], BF16, name="wraw%d%d%d" % (w, c, hf))
                    nc.sync.dma_start(out=t[:], in_=wsrc[:, 2 * hf : 2 * hf + 2, :])
                    wr.extend([t[:, 0, :], t[:, 1, :]])
                rows.append(wr)

        ident = const.tile([P, P], F32, name="ident")
        make_identity(nc, ident[:])
        one1 = small.tile([P, 1], F32, name="one1")
        nc.vector.memset(one1[:], 1.0)
        one2 = small.tile([P, 1], F32, name="one2")
        nc.scalar.activation(out=one2[:], in_=one1[:], func=ACT.Sqrt)

        ops = {}
        queues = {"PE": [], "V": [], "S": [], "SP": []}

        def add(eng, key, name, deps, emit, takes=(), frees=()):
            ops[name] = (deps, emit, takes, frees)
            queues[eng].append((key, len(ops), name))

        tiles = {}

        def copy_on(eng, out, in_):
            if eng == "V":
                nc.vector.tensor_copy(out=out, in_=in_)
            else:
                nc.scalar.copy(out=out, in_=in_)

        def emit_bmm(w):
            pb = accp.tile([P, E], BF16, tag="acc", name="pb%d" % w)
            tiles[("pb", w)] = pb
            for c in range(2):
                nc.tensor.matmul(
                    out=pb[:, c * NBLK : (c + 1) * NBLK],
                    lhsT=ones[:],
                    rhs=bzs[w][:, c * NBLK : (c + 1) * NBLK],
                    start=True,
                    stop=True,
                )

        def emit_bc(w):
            bb = const.tile([P, E], BF16, name="bias%d" % w)
            tiles[("bias", w)] = bb
            copy_on(BC_ENG[w], bb[:], tiles[("pb", w)][:])

        def emit_warm(i, n):
            pd = accp.tile([P, NBLK], F32, tag="acc", name="warm%d" % i)
            for k in range(n):
                nc.tensor.matmul(out=pd[:], lhsT=ones[:], rhs=dz[:], start=True, stop=True)

        for i, (key, n) in enumerate(WARM):
            add("PE", key, "D%d" % i, (), lambda i=i, n=n: emit_warm(i, n), takes=("acc",), frees=("acc",))

        for w in range(3):
            add("PE", KB[w], "bmm%d" % w, (), lambda w=w: emit_bmm(w), takes=("acc",))
            add(BC_ENG[w], KB[w] + 0.3, "bc%d" % w, ("bmm%d" % w,), lambda w=w: emit_bc(w), frees=("acc",))

        def emit_t(blk, r):
            if r == 0:
                tiles[("g4", blk)] = grp.tile(
                    [P, 2, NBLK, 4], BF16, tag="g4", name="g4_%d" % blk, align_bytes=64
                )
            tp = tpp.tile([P, 2, 2, P], F32, tag="tp", name="tp%d_%d" % (blk, r))
            tiles[("tp", blk, r)] = tp
            src = rows[blk][r].bitcast(F32)
            for g in range(2):
                for u in range(2):
                    k0 = 256 * g + 128 * u
                    nc.tensor.transpose(tp[:, g, u, :], src[:, k0 : k0 + P], ident[:])

        def emit_e(blk, r, eng):
            gw = tiles[("g4", blk)][:].bitcast(F32)
            copy_on(
                eng,
                gw[:, :, r * P : (r + 1) * P, :],
                tiles[("tp", blk, r)][:].rearrange("p g u r -> p g r u"),
            )

        def emit_q(blk, g):
            if g == 0:
                tiles[("cd", blk)] = keep.tile([P, 2, NBLK], U32, name="cd%d" % blk, align_bytes=64)
                tiles[("pl", blk)] = keep.tile([P, 2, NBLK], U8, name="pl%d" % blk, align_bytes=64)
            nc.vector.quantize_mx(
                out=tiles[("cd", blk)][:, g, :].bitcast(FP8X4),
                scales=tiles[("pl", blk)][:, g, :],
                in_=tiles[("g4", blk)][:, g, :, :].rearrange("p f t -> p (f t)"),
            )

        for blk in range(7):
            for r in range(4):
                if blk <= 2:
                    kt = -100.0 + 4 * blk + r
                    ke = kt
                else:
                    j = 4 * (blk - 3) + r
                    kt = TRUN * (j // TRUN) - LEAD_T + 0.01 * j - 0.5
                    ke = j - LEAD_E
                eng = "V" if r in VEC_E[blk] else "S"
                add(
                    "PE", kt, "T%d.%d" % (blk, r), (), lambda blk=blk, r=r: emit_t(blk, r),
                    takes=("tp", "grp") if r == 0 else ("tp",),
                )
                add(
                    eng, ke + 0.001, "E%d.%d" % (blk, r), ("T%d.%d" % (blk, r),),
                    lambda blk=blk, r=r, eng=eng: emit_e(blk, r, eng), frees=("tp",),
                )
            for g in range(2):
                if blk <= 2:
                    kq = -100.0 + 4 * blk + 3.5 + 0.1 * g
                else:
                    kq = 4 * (blk - 3) + 3 - LEAD_E + DQ + 0.1 * g
                add(
                    "V", kq, "Q%d.%d" % (blk, g), tuple("E%d.%d" % (blk, r) for r in range(4)),
                    lambda blk=blk, g=g: emit_q(blk, g), frees=("grp",) if g == 1 else (),
                )

        def emit_m(blk, tt):
            acc = accp.tile([P, NBLK], F32, tag="acc", name="acc%d_%d" % (blk, tt))
            tiles[("acc", blk, tt)] = acc
            for g in range(2):
                nc.tensor.matmul_mx(
                    out=acc[:],
                    lhsT=tiles[("cd", 0)][:, g, tt * P : (tt + 1) * P].bitcast(FP8X4),
                    lhsT_scale=tiles[("pl", 0)][:, g, tt * P : (tt + 1) * P],
                    rhs=tiles[("cd", blk)][:, g, :].bitcast(FP8X4),
                    rhs_scale=tiles[("pl", blk)][:, g, :],
                    start=(g == 0),
                    stop=(g == 1),
                )

        def emit_a(blk, tt):
            w, c = divmod(blk - 1, 2)
            b, jj = divmod(tt, 2)
            if (w, b) not in tiles:
                tiles[(w, b)] = res.tile([P, 8, 2, P], F32, name="o%d%d" % (w, b))
            y = tiles[(w, b)][:, 4 * c : 4 * c + 4, jj, :]
            nc.vector.tensor_tensor(
                out=y.rearrange("p h (e r) -> p h e r", r=4),
                in0=tiles[("acc", blk, tt)][:].rearrange("p (r h e) -> p h e r", r=4, h=4),
                in1=tiles[("bias", w)][:, c * NBLK : (c + 1) * NBLK].rearrange(
                    "p (h e r) -> p h e r", h=4, r=4
                ),
                op=ALU.add,
            )

        def emit_sq(w, tt):
            b, jj = divmod(tt, 2)
            if ("ss", w) not in tiles:
                tiles[("ss", w)] = small.tile([P, 4], F32, name="ss%d" % w)
            junk = scr.tile([P, 8, P], F32, tag="junk", name="junk%d_%d" % (w, tt))
            nc.scalar.activation(
                out=junk[:], in_=tiles[(w, b)][:, :, jj, :], func=ACT.Square,
                accum_out=tiles[("ss", w)][:, tt : tt + 1],
            )

        def emit_n(step, w, b):
            if step == 2:
                m2 = small.tile([P, 2], F32, name="m2_%d%d" % (w, b))
                tiles[("m2", w, b)] = m2
                nc.vector.tensor_scalar(
                    out=m2[:], in0=tiles[("ss", w)][:, 2 * b : 2 * b + 2], scalar1=1e-24, scalar2=None,
                    op0=ALU.max,
                )
            elif step == 3:
                n2 = small.tile([P, 2], F32, name="n2_%d%d" % (w, b))
                tiles[("n2", w, b)] = n2
                nc.scalar.activation(out=n2[:], in_=tiles[("m2", w, b)][:], func=ACT.Sqrt)
            else:
                r2 = small.tile([P, 2], F32, name="r2_%d%d" % (w, b))
                tiles[("r2", w, b)] = r2
                nc.vector.reciprocal(out=r2[:], in_=tiles[("n2", w, b)][:])

        def emit_r(w, tt, eng):
            b, jj = divmod(tt, 2)
            y = tiles[(w, b)][:, :, jj, :]
            rr = tiles[("r2", w, b)][:, jj : jj + 1]
            if eng == "V":
                nc.vector.tensor_scalar(out=y, in0=y, scalar1=rr, scalar2=None, op0=ALU.mult)
            else:
                nc.scalar.activation(out=y, in_=y, func=ACT.Copy, scale=rr)

        def emit_store(w, b, h0, h1):
            nc.sync.dma_start(
                out=outs[w][b, h0:h1].rearrange("h (p j) d -> p h (j d)", j=2),
                in_=tiles[(w, b)][:, h0:h1, :, :].rearrange("p h j d -> p h (j d)"),
            )

        units = [
            (2 * w + 1 + c, 2 * b + jj)
            for w in range(3) for b in range(2) for c in range(2) for jj in range(2)
        ]
        slot = {}
        for i, (blk, tt) in enumerate(units):
            slot[(blk, tt)] = i
            w = (blk - 1) // 2
            add(
                "PE", float(i), "M%d.%d" % (blk, tt), ("Q0.0", "Q0.1", "Q%d.0" % blk, "Q%d.1" % blk),
                lambda blk=blk, tt=tt: emit_m(blk, tt), takes=("acc",),
            )
            add(
                "V", i + 0.2, "A%d.%d" % (blk, tt), ("M%d.%d" % (blk, tt), "bc%d" % w),
                lambda blk=blk, tt=tt: emit_a(blk, tt), frees=("acc",),
            )
        for w in range(2):
            for b in range(2):
                last = 0
                for tt in (2 * b, 2 * b + 1):
                    j = max(slot[(2 * w + 1, tt)], slot[(2 * w + 2, tt)])
                    last = max(last, j)
                    add(
                        "S", j + DS, "Sq%d.%d" % (w, tt), ("A%d.%d" % (2 * w + 1, tt), "A%d.%d" % (2 * w + 2, tt)),
                        lambda w=w, tt=tt: emit_sq(w, tt),
                    )
                t = "%d%d" % (w, b)
                add("V", last + DN, "N2." + t, ("Sq%d.%d" % (w, 2 * b), "Sq%d.%d" % (w, 2 * b + 1)),
                    lambda w=w, b=b: emit_n(2, w, b))
                add("S", last + DN + 0.05, "N3." + t, ("N2." + t,), lambda w=w, b=b: emit_n(3, w, b))
                add("V", last + DN + DN4, "N4." + t, ("N3." + t,), lambda w=w, b=b: emit_n(4, w, b))
                for q, tt in enumerate((2 * b, 2 * b + 1)):
                    add(
                        R_ENG[q], last + DN + DN4 + 0.01 + q * DR, "R%d.%d" % (w, tt), ("N4." + t,),
                        lambda w=w, tt=tt, q=q: emit_r(w, tt, R_ENG[q]),
                    )
                for c in range(2):
                    add("SP", last + 3.0 + 0.1 * c, "St%s%d" % (t, c), ("R%d.%d" % (w, 2 * b), "R%d.%d" % (w, 2 * b + 1)),
                        lambda w=w, b=b, c=c: emit_store(w, b, 4 * c, 4 * c + 4))
        for c in range(2):
            for b in range(2):
                add(
                    "SP", float(slot[(5 + c, 2 * b + 1)]), "Stv%d%d" % (c, b),
                    ("A%d.%d" % (5 + c, 2 * b), "A%d.%d" % (5 + c, 2 * b + 1)),
                    lambda c=c, b=b: emit_store(2, b, 4 * c, 4 * c + 4),
                )

        order = {e: [n for (k, i, n) in sorted(q)] for e, q in queues.items()}
        head = {e: 0 for e in order}
        done = set()
        held = {"tp": 0, "acc": 0, "grp": 0}
        left = len(ops)
        while left:
            moved = False
            for e in ("PE", "S", "V", "SP"):
                while head[e] < len(order[e]):
                    name = order[e][head[e]]
                    deps, emit, takes, frees = ops[name]
                    if not all(d in done for d in deps):
                        break
                    if not all(held[p] < BUFS[p] for p in takes):
                        break
                    emit()
                    for p in takes:
                        held[p] += 1
                    for p in frees:
                        held[p] -= 1
                    done.add(name)
                    head[e] += 1
                    left -= 1
                    moved = True
            assert moved, "the orders of the engines block each other"
